import numpy as np
import ml_dtypes

BF16 = ml_dtypes.bfloat16


def bf(x):
    return np.asarray(x, np.float32).astype(BF16)


def f32(x):
    return np.asarray(x, np.float32)


def f64(x):
    return np.asarray(x).astype(np.float64)


def striped(idx):
    return np.tile(idx.reshape(-1, 16).T, (8, 1))


C, S, L, K, Q, N = 128, 2048, 512, 3, 4, 1536
EPS = 1e-5


def mish(v):
    return v * np.tanh(np.log(1.0 + np.exp(v)))


def setup_inputs():
    return {"x": f32(np.random.standard_normal((C, S))), "own": f32(np.random.standard_normal((C, L))), "w1": bf(np.random.standard_normal((C, C)) / np.sqrt(C)), "b1": f32(0.1 * np.random.standard_normal((C, 1))), "w2": bf(np.random.standard_normal((C, C)) / np.sqrt(C)), "b2": f32(0.1 * np.random.standard_normal((C, 1))), "gamma": f32(1.0 + 0.1 * np.random.standard_normal((C, 1))), "beta": f32(0.1 * np.random.standard_normal((C, 1))), "offs": striped(np.random.permutation(np.tile(np.arange(S), 2))[:N])}


def reference(x, own, w1, b1, w2, b2, gamma, beta, offs):
    idx = offs[:16].T.reshape(-1)
    ctx = (f64(own) + f64(x)[:, idx].reshape(C, K, L).sum(axis=1)) / Q
    h = mish(f64(w1).T @ ctx + f64(b1))
    res = f64(own) + f64(w2).T @ h + f64(b2)
    mu = res.mean(axis=0, keepdims=True)
    var = ((res - mu) ** 2).mean(axis=0, keepdims=True)
    return (res - mu) / np.sqrt(var + EPS) * f64(gamma) + f64(beta)

@@ -1,0 +1,118 @@
+import concourse.mybir as mybir
+from concourse.masks import make_identity
+
+F32, BF16, U16 = mybir.dt.float32, mybir.dt.bfloat16, mybir.dt.uint16
+ADD, SUBTRACT, MULT = mybir.AluOpType.add, mybir.AluOpType.subtract, mybir.AluOpType.mult
+FUNC = mybir.ActivationFunctionType
+
+C = 128
+S = 2048
+L = 512
+K = 3
+CHUNK = 256
+BLOCK = 128
+EPS = 1e-5
+FLOPS = 2 * 2 * C * C * L
+
+
+def tile_hybridtriaxialblock_kernel(tc, x, own, w1, b1, w2, b2, gamma, beta, offs, out):
+    nc = tc.nc
+    with (
+        tc.tile_pool(name="held", bufs=1) as held,
+        tc.tile_pool(name="work", bufs=2) as work,
+        tc.tile_pool(name="small", bufs=4) as small,
+        tc.psum_pool(name="res_banks", bufs=1) as res_banks,
+        tc.psum_pool(name="banks", bufs=4) as banks,
+    ):
+        offsets = held.tile([C, K * L // 16], U16, name="offsets")
+        nc.sync.dma_start(offsets[:], offs)
+        own_sb = held.tile([C, L], F32, name="own_sb")
+        nc.sync.dma_start(own_sb[:], own)
+        x_sb = held.tile([C, S], F32, name="x_sb")
+        nc.sync.dma_start(x_sb[:], x)
+        w1_sb = held.tile([C, C], BF16, name="w1_sb")
+        nc.scalar.dma_start(w1_sb[:], w1)
+        w2_sb = held.tile([C, C], BF16, name="w2_sb")
+        nc.scalar.dma_start(w2_sb[:], w2)
+        rows = held.tile([4, C], F32, name="rows")
+        for k, vector in enumerate((b1, b2, gamma, beta)):
+            nc.gpsimd.dma_start(rows[k : k + 1, :], vector.rearrange("c one -> one c"))
+
+        ident = held.tile([C, C], F32, name="ident")
+        make_identity(nc, ident[:])
+        zero_col = held.tile([C, 1], F32, name="zero_col")
+        nc.vector.memset(zero_col[:], 0.0)
+        two_col = held.tile([C, 1], F32, name="two_col")
+        nc.vector.memset(two_col[:], 2.0)
+        eps_col = held.tile([C, 1], F32, name="eps_col")
+        nc.vector.memset(eps_col[:], EPS)
+        warm = held.tile([C, 1], F32, name="warm")
+        nc.scalar.activation(warm[:], zero_col[:], FUNC.Sigmoid)
+
+        cols_ps = banks.tile([C, 4], F32, name="cols_ps", tag="bank")
+        nc.tensor.matmul(cols_ps[:], lhsT=rows[:], rhs=ident[0:4, 0:4], start=True, stop=True)
+        cols = held.tile([C, 4], F32, name="cols")
+        nc.vector.tensor_copy(cols[:], cols_ps[:])
+        b1_col, b2_col, gamma_col, beta_col = (cols[:, k : k + 1] for k in range(4))
+
+        own_b2 = held.tile([C, L], F32, name="own_b2")
+        nc.scalar.activation(own_b2[:], own_sb[:], FUNC.Identity, bias=b2_col)
+        res_t = []
+        for b in range(L // BLOCK):
+            bank = res_banks.tile([BLOCK, C], F32, name=f"res_t{b}")
+            nc.tensor.matmul(
+                bank[:], lhsT=own_b2[:, b * BLOCK : (b + 1) * BLOCK], rhs=ident[:], start=True, stop=False
+            )
+            res_t.append(bank)
+
+        sig = held.tile([C, L], F32, name="sig")
+        v_ps = []
+        for c in range(L // CHUNK):
+            lines = slice(c * CHUNK, (c + 1) * CHUNK)
+            total = own_sb[:, lines]
+            for k in range(K):
+                first = (k * L + c * CHUNK) // 16
+                picked = x_sb[:].indirect(offsets[:, first : first + CHUNK // 16])
+                longer = work.tile([C, CHUNK], F32, name=f"sum{k}")
+                nc.vector.tensor_tensor(longer[:], picked, total, ADD)
+                total = longer[:]
+            ctx = work.tile([C, CHUNK], BF16, name="ctx")
+            nc.scalar.activation(ctx[:], total, FUNC.Copy, scale=0.25)
+            v_bank = banks.tile([C, CHUNK], F32, name="v_bank", tag="bank")
+            nc.tensor.matmul(v_bank[:], lhsT=w1_sb[:], rhs=ctx[:], start=True, stop=True)
+            nc.scalar.activation(sig[:, lines], v_bank[:], FUNC.Sigmoid, bias=b1_col)
+            v_ps.append(v_bank)
+
+        neg_t = held.tile([C, L], F32, name="neg_t")
+        nc.vector.scalar_tensor_tensor(neg_t[:], in0=sig[:], scalar=2.0, in1=sig[:], op0=SUBTRACT, op1=MULT)
+        for c in range(L // CHUNK):
+            lines = slice(c * CHUNK, (c + 1) * CHUNK)
+            neg_vt = work.tile([C, CHUNK], F32, name="neg_vt")
+            nc.vector.scalar_tensor_tensor(
+                neg_vt[:], in0=v_ps[c][:], scalar=b1_col, in1=neg_t[:, lines], op0=ADD, op1=MULT
+            )
+            root = work.tile([C, CHUNK], F32, name="root")
+            nc.scalar.activation(root[:], neg_t[:, lines], FUNC.Abs_reciprocal_sqrt, bias=two_col[:])
+            recip = work.tile([C, CHUNK], F32, name="recip")
+            nc.scalar.activation(recip[:], root[:], FUNC.Square)
+            h = work.tile([C, CHUNK], BF16, name="h")
+            nc.vector.scalar_tensor_tensor(h[:], in0=neg_vt[:], scalar=-1.0, in1=recip[:], op0=MULT, op1=MULT)
+
+            for b in range(c * CHUNK // BLOCK, (c + 1) * CHUNK // BLOCK):
+                inside = slice(b * BLOCK - c * CHUNK, (b + 1) * BLOCK - c * CHUNK)
+                nc.tensor.matmul(res_t[b][:], lhsT=h[:, inside], rhs=w2_sb[:], start=False, stop=True)
+                stats = small.tile([BLOCK, 6], F32, name="stats")
+                nc.vector.bn_stats(stats[:], res_t[b][:])
+                mean_var = small.tile([BLOCK, 2], F32, name="mean_var")
+                nc.vector.bn_aggr(mean_var[:], stats[:])
+                rstd = small.tile([BLOCK, 1], F32, name="rstd")
+                nc.scalar.activation(rstd[:], mean_var[:, 1:2], FUNC.Abs_reciprocal_sqrt, bias=eps_col[:])
+                normed = work.tile([BLOCK, C], F32, name="normed")
+                nc.vector.tensor_scalar(
+                    normed[:], res_t[b][:], mean_var[:, 0:1], rstd[:], op0=SUBTRACT, op1=MULT
+                )
+                back = banks.tile([C, BLOCK], F32, name="back", tag="bank")
+                nc.tensor.transpose(back[:], normed[:], ident[:])
+                result = work.tile([C, BLOCK], F32, name="result")
+                nc.scalar.activation(result[:], back[:], FUNC.Identity, scale=gamma_col, bias=beta_col)
+                nc.sync.dma_start(out[:, b * BLOCK : (b + 1) * BLOCK], result[:])

@@ -9,7 +9,7 @@ C = 128
 S = 2048
 L = 512
 K = 3
-CHUNK = 256
+CHUNKS = ((0, 384), (384, 128))
 BLOCK = 128
 EPS = 1e-5
 FLOPS = 2 * 2 * C * C * L
@@ -19,7 +19,7 @@ def tile_hybridtriaxialblock_kernel(tc, x, own, w1, b1, w2, b2, gamma, beta, off
     nc = tc.nc
     with (
         tc.tile_pool(name="held", bufs=1) as held,
-        tc.tile_pool(name="work", bufs=2) as work,
+        tc.tile_pool(name="work", bufs=4) as work,
         tc.tile_pool(name="small", bufs=4) as small,
         tc.psum_pool(name="res_banks", bufs=1) as res_banks,
         tc.psum_pool(name="banks", bufs=4) as banks,
@@ -30,20 +30,21 @@ def tile_hybridtriaxialblock_kernel(tc, x, own, w1, b1, w2, b2, gamma, beta, off
         nc.sync.dma_start(own_sb[:], own)
         x_sb = held.tile([C, S], F32, name="x_sb")
         nc.sync.dma_start(x_sb[:], x)
+        rows = held.tile([4, C], F32, name="rows")
+        for k, vector in enumerate((b1, b2, gamma, beta)):
+            nc.scalar.dma_start(rows[k : k + 1, :], vector.rearrange("c one -> one c"))
         w1_sb = held.tile([C, C], BF16, name="w1_sb")
         nc.scalar.dma_start(w1_sb[:], w1)
         w2_sb = held.tile([C, C], BF16, name="w2_sb")
         nc.scalar.dma_start(w2_sb[:], w2)
-        rows = held.tile([4, C], F32, name="rows")
-        for k, vector in enumerate((b1, b2, gamma, beta)):
-            nc.gpsimd.dma_start(rows[k : k + 1, :], vector.rearrange("c one -> one c"))
 
         ident = held.tile([C, C], F32, name="ident")
-        make_identity(nc, ident[:])
+        nc.vector.memset(ident[:], 0.0)
+        make_identity(nc, ident[:], nomemset=True)
         zero_col = held.tile([C, 1], F32, name="zero_col")
         nc.vector.memset(zero_col[:], 0.0)
-        two_col = held.tile([C, 1], F32, name="two_col")
-        nc.vector.memset(two_col[:], 2.0)
+        four_col = held.tile([C, 1], F32, name="four_col")
+        nc.vector.memset(four_col[:], 4.0)
         eps_col = held.tile([C, 1], F32, name="eps_col")
         nc.vector.memset(eps_col[:], EPS)
         warm = held.tile([C, 1], F32, name="warm")
@@ -67,52 +68,56 @@ def tile_hybridtriaxialblock_kernel(tc, x, own, w1, b1, w2, b2, gamma, beta, off
 
         sig = held.tile([C, L], F32, name="sig")
         v_ps = []
-        for c in range(L // CHUNK):
-            lines = slice(c * CHUNK, (c + 1) * CHUNK)
+        for c, (start, width) in enumerate(CHUNKS):
+            lines = slice(start, start + width)
             total = own_sb[:, lines]
             for k in range(K):
-                first = (k * L + c * CHUNK) // 16
-                picked = x_sb[:].indirect(offsets[:, first : first + CHUNK // 16])
-                longer = work.tile([C, CHUNK], F32, name=f"sum{k}")
+                first = (k * L + start) // 16
+                picked = x_sb[:].indirect(offsets[:, first : first + width // 16])
+                longer = held.tile([C, width], F32, name=f"sum{k}_{c}")
                 nc.vector.tensor_tensor(longer[:], picked, total, ADD)
                 total = longer[:]
-            ctx = work.tile([C, CHUNK], BF16, name="ctx")
+            ctx = held.tile([C, width], BF16, name=f"ctx{c}")
             nc.scalar.activation(ctx[:], total, FUNC.Copy, scale=0.25)
-            v_bank = banks.tile([C, CHUNK], F32, name="v_bank", tag="bank")
+            v_bank = banks.tile([C, width], F32, name=f"v_bank{c}", tag="bank")
             nc.tensor.matmul(v_bank[:], lhsT=w1_sb[:], rhs=ctx[:], start=True, stop=True)
             nc.scalar.activation(sig[:, lines], v_bank[:], FUNC.Sigmoid, bias=b1_col)
             v_ps.append(v_bank)
 
         neg_t = held.tile([C, L], F32, name="neg_t")
-        nc.vector.scalar_tensor_tensor(neg_t[:], in0=sig[:], scalar=2.0, in1=sig[:], op0=SUBTRACT, op1=MULT)
-        for c in range(L // CHUNK):
-            lines = slice(c * CHUNK, (c + 1) * CHUNK)
-            neg_vt = work.tile([C, CHUNK], F32, name="neg_vt")
+        neg_vt = held.tile([C, L], F32, name="neg_vt")
+        for c, (start, width) in enumerate(CHUNKS):
+            lines = slice(start, start + width)
             nc.vector.scalar_tensor_tensor(
-                neg_vt[:], in0=v_ps[c][:], scalar=b1_col, in1=neg_t[:, lines], op0=ADD, op1=MULT
+                neg_t[:, lines], in0=sig[:, lines], scalar=2.0, in1=sig[:, lines], op0=SUBTRACT, op1=MULT
             )
-            root = work.tile([C, CHUNK], F32, name="root")
-            nc.scalar.activation(root[:], neg_t[:, lines], FUNC.Abs_reciprocal_sqrt, bias=two_col[:])
-            recip = work.tile([C, CHUNK], F32, name="recip")
-            nc.scalar.activation(recip[:], root[:], FUNC.Square)
-            h = work.tile([C, CHUNK], BF16, name="h")
-            nc.vector.scalar_tensor_tensor(h[:], in0=neg_vt[:], scalar=-1.0, in1=recip[:], op0=MULT, op1=MULT)
+            nc.vector.scalar_tensor_tensor(
+                neg_vt[:, lines], in0=v_ps[c][:], scalar=b1_col, in1=neg_t[:, lines], op0=ADD, op1=MULT
+            )
+        square_less_4 = held.tile([C, L], F32, name="square_less_4")
+        nc.vector.scalar_tensor_tensor(
+            square_less_4[:], in0=neg_t[:], scalar=4.0, in1=neg_t[:], op0=ADD, op1=MULT
+        )
 
-            for b in range(c * CHUNK // BLOCK, (c + 1) * CHUNK // BLOCK):
-                inside = slice(b * BLOCK - c * CHUNK, (b + 1) * BLOCK - c * CHUNK)
-                nc.tensor.matmul(res_t[b][:], lhsT=h[:, inside], rhs=w2_sb[:], start=False, stop=True)
-                stats = small.tile([BLOCK, 6], F32, name="stats")
-                nc.vector.bn_stats(stats[:], res_t[b][:])
-                mean_var = small.tile([BLOCK, 2], F32, name="mean_var")
-                nc.vector.bn_aggr(mean_var[:], stats[:])
-                rstd = small.tile([BLOCK, 1], F32, name="rstd")
-                nc.scalar.activation(rstd[:], mean_var[:, 1:2], FUNC.Abs_reciprocal_sqrt, bias=eps_col[:])
-                normed = work.tile([BLOCK, C], F32, name="normed")
-                nc.vector.tensor_scalar(
-                    normed[:], res_t[b][:], mean_var[:, 0:1], rstd[:], op0=SUBTRACT, op1=MULT
-                )
-                back = banks.tile([C, BLOCK], F32, name="back", tag="bank")
-                nc.tensor.transpose(back[:], normed[:], ident[:])
-                result = work.tile([C, BLOCK], F32, name="result")
-                nc.scalar.activation(result[:], back[:], FUNC.Identity, scale=gamma_col, bias=beta_col)
-                nc.sync.dma_start(out[:, b * BLOCK : (b + 1) * BLOCK], result[:])
+        for b in range(L // BLOCK):
+            lines = slice(b * BLOCK, (b + 1) * BLOCK)
+            recip = work.tile([C, BLOCK], F32, name="recip")
+            nc.scalar.activation(recip[:], square_less_4[:, lines], FUNC.Abs_reciprocal_sqrt, bias=four_col[:])
+            h = work.tile([C, BLOCK], BF16, name="h")
+            nc.vector.scalar_tensor_tensor(
+                h[:], in0=neg_vt[:, lines], scalar=-1.0, in1=recip[:], op0=MULT, op1=MULT
+            )
+            nc.tensor.matmul(res_t[b][:], lhsT=h[:], rhs=w2_sb[:], start=False, stop=True)
+            stats = small.tile([BLOCK, 6], F32, name="stats")
+            nc.vector.bn_stats(stats[:], res_t[b][:])
+            mean_var = small.tile([BLOCK, 2], F32, name="mean_var")
+            nc.vector.bn_aggr(mean_var[:], stats[:])
+            rstd = small.tile([BLOCK, 1], F32, name="rstd")
+            nc.scalar.activation(rstd[:], mean_var[:, 1:2], FUNC.Abs_reciprocal_sqrt, bias=eps_col[:])
+            normed = work.tile([BLOCK, C], F32, name="normed")
+            nc.vector.tensor_scalar(normed[:], res_t[b][:], mean_var[:, 0:1], rstd[:], op0=SUBTRACT, op1=MULT)
+            back = banks.tile([C, BLOCK], F32, name="back", tag="bank")
+            nc.tensor.transpose(back[:], normed[:], ident[:])
+            result = work.tile([C, BLOCK], F32, name="result")
+            nc.scalar.activation(result[:], back[:], FUNC.Identity, scale=gamma_col, bias=beta_col)
+            nc.sync.dma_start(out[:, lines], result[:])

@@ -9,7 +9,7 @@ C = 128
 S = 2048
 L = 512
 K = 3
-CHUNKS = ((0, 384), (384, 128))
+CHUNKS = ((0, 256), (256, 256))
 BLOCK = 128
 EPS = 1e-5
 FLOPS = 2 * 2 * C * C * L

@@ -26,10 +26,10 @@ def tile_hybridtriaxialblock_kernel(tc, x, own, w1, b1, w2, b2, gamma, beta, off
     ):
         offsets = held.tile([C, K * L // 16], U16, name="offsets")
         nc.sync.dma_start(offsets[:], offs)
-        own_sb = held.tile([C, L], F32, name="own_sb")
-        nc.sync.dma_start(own_sb[:], own)
         x_sb = held.tile([C, S], F32, name="x_sb")
         nc.sync.dma_start(x_sb[:], x)
+        own_sb = held.tile([C, L], F32, name="own_sb")
+        nc.scalar.dma_start(own_sb[:], own)
         rows = held.tile([4, C], F32, name="rows")
         for k, vector in enumerate((b1, b2, gamma, beta)):
             nc.scalar.dma_start(rows[k : k + 1, :], vector.rearrange("c one -> one c"))

@@ -24,10 +24,10 @@ def tile_hybridtriaxialblock_kernel(tc, x, own, w1, b1, w2, b2, gamma, beta, off
         tc.psum_pool(name="res_banks", bufs=1) as res_banks,
         tc.psum_pool(name="banks", bufs=4) as banks,
     ):
-        offsets = held.tile([C, K * L // 16], U16, name="offsets")
-        nc.sync.dma_start(offsets[:], offs)
         x_sb = held.tile([C, S], F32, name="x_sb")
         nc.sync.dma_start(x_sb[:], x)
+        offsets = held.tile([C, K * L // 16], U16, name="offsets")
+        nc.sync.dma_start(offsets[:], offs)
         own_sb = held.tile([C, L], F32, name="own_sb")
         nc.scalar.dma_start(own_sb[:], own)
         rows = held.tile([4, C], F32, name="rows")

import concourse.mybir as mybir
from concourse.masks import make_identity

F32, BF16, U16 = mybir.dt.float32, mybir.dt.bfloat16, mybir.dt.uint16
ADD, SUBTRACT, MULT = mybir.AluOpType.add, mybir.AluOpType.subtract, mybir.AluOpType.mult
FUNC = mybir.ActivationFunctionType

C = 128
S = 2048
L = 512
K = 3
CHUNKS = ((0, 256), (256, 256))
BLOCK = 128
EPS = 1e-5
FLOPS = 2 * 2 * C * C * L


def tile_hybridtriaxialblock_kernel(tc, x, own, w1, b1, w2, b2, gamma, beta, offs, out):
    nc = tc.nc
    with (
        tc.tile_pool(name="held", bufs=1) as held,
        tc.tile_pool(name="work", bufs=4) as work,
        tc.tile_pool(name="small", bufs=4) as small,
        tc.psum_pool(name="res_banks", bufs=1) as res_banks,
        tc.psum_pool(name="banks", bufs=4) as banks,
    ):
        x_sb = held.tile([C, S], F32, name="x_sb")
        nc.sync.dma_start(x_sb[:], x)
        offsets = held.tile([C, K * L // 16], U16, name="offsets")
        nc.sync.dma_start(offsets[:], offs)
        own_sb = held.tile([C, L], F32, name="own_sb")
        nc.scalar.dma_start(own_sb[:], own)
        rows = held.tile([4, C], F32, name="rows")
        for k, vector in enumerate((b1, b2, gamma, beta)):
            nc.scalar.dma_start(rows[k : k + 1, :], vector.rearrange("c one -> one c"))
        w1_sb = held.tile([C, C], BF16, name="w1_sb")
        nc.scalar.dma_start(w1_sb[:], w1)
        w2_sb = held.tile([C, C], BF16, name="w2_sb")
        nc.scalar.dma_start(w2_sb[:], w2)

        ident = held.tile([C, C], F32, name="ident")
        nc.vector.memset(ident[:], 0.0)
        make_identity(nc, ident[:], nomemset=True)
        zero_col = held.tile([C, 1], F32, name="zero_col")
        nc.vector.memset(zero_col[:], 0.0)
        four_col = held.tile([C, 1], F32, name="four_col")
        nc.vector.memset(four_col[:], 4.0)
        eps_col = held.tile([C, 1], F32, name="eps_col")
        nc.vector.memset(eps_col[:], EPS)
        warm = held.tile([C, 1], F32, name="warm")
        nc.scalar.activation(warm[:], zero_col[:], FUNC.Sigmoid)

        cols_ps = banks.tile([C, 4], F32, name="cols_ps", tag="bank")
        nc.tensor.matmul(cols_ps[:], lhsT=rows[:], rhs=ident[0:4, 0:4], start=True, stop=True)
        cols = held.tile([C, 4], F32, name="cols")
        nc.vector.tensor_copy(cols[:], cols_ps[:])
        b1_col, b2_col, gamma_col, beta_col = (cols[:, k : k + 1] for k in range(4))

        own_b2 = held.tile([C, L], F32, name="own_b2")
        nc.scalar.activation(own_b2[:], own_sb[:], FUNC.Identity, bias=b2_col)
        res_t = []
        for b in range(L // BLOCK):
            bank = res_banks.tile([BLOCK, C], F32, name=f"res_t{b}")
            nc.tensor.matmul(
                bank[:], lhsT=own_b2[:, b * BLOCK : (b + 1) * BLOCK], rhs=ident[:], start=True, stop=False
            )
            res_t.append(bank)

        sig = held.tile([C, L], F32, name="sig")
        v_ps = []
        for c, (start, width) in enumerate(CHUNKS):
            lines = slice(start, start + width)
            total = own_sb[:, lines]
            for k in range(K):
                first = (k * L + start) // 16
                picked = x_sb[:].indirect(offsets[:, first : first + width // 16])
                longer = held.tile([C, width], F32, name=f"sum{k}_{c}")
                nc.vector.tensor_tensor(longer[:], picked, total, ADD)
                total = longer[:]
            ctx = held.tile([C, width], BF16, name=f"ctx{c}")
            nc.scalar.activation(ctx[:], total, FUNC.Copy, scale=0.25)
            v_bank = banks.tile([C, width], F32, name=f"v_bank{c}", tag="bank")
            nc.tensor.matmul(v_bank[:], lhsT=w1_sb[:], rhs=ctx[:], start=True, stop=True)
            nc.scalar.activation(sig[:, lines], v_bank[:], FUNC.Sigmoid, bias=b1_col)
            v_ps.append(v_bank)

        neg_t = held.tile([C, L], F32, name="neg_t")
        neg_vt = held.tile([C, L], F32, name="neg_vt")
        for c, (start, width) in enumerate(CHUNKS):
            lines = slice(start, start + width)
            nc.vector.scalar_tensor_tensor(
                neg_t[:, lines], in0=sig[:, lines], scalar=2.0, in1=sig[:, lines], op0=SUBTRACT, op1=MULT
            )
            nc.vector.scalar_tensor_tensor(
                neg_vt[:, lines], in0=v_ps[c][:], scalar=b1_col, in1=neg_t[:, lines], op0=ADD, op1=MULT
            )
        square_less_4 = held.tile([C, L], F32, name="square_less_4")
        nc.vector.scalar_tensor_tensor(
            square_less_4[:], in0=neg_t[:], scalar=4.0, in1=neg_t[:], op0=ADD, op1=MULT
        )

        for b in range(L // BLOCK):
            lines = slice(b * BLOCK, (b + 1) * BLOCK)
            recip = work.tile([C, BLOCK], F32, name="recip")
            nc.scalar.activation(recip[:], square_less_4[:, lines], FUNC.Abs_reciprocal_sqrt, bias=four_col[:])
            h = work.tile([C, BLOCK], BF16, name="h")
            nc.vector.scalar_tensor_tensor(
                h[:], in0=neg_vt[:, lines], scalar=-1.0, in1=recip[:], op0=MULT, op1=MULT
            )
            nc.tensor.matmul(res_t[b][:], lhsT=h[:], rhs=w2_sb[:], start=False, stop=True)
            stats = small.tile([BLOCK, 6], F32, name="stats")
            nc.vector.bn_stats(stats[:], res_t[b][:])
            mean_var = small.tile([BLOCK, 2], F32, name="mean_var")
            nc.vector.bn_aggr(mean_var[:], stats[:])
            rstd = small.tile([BLOCK, 1], F32, name="rstd")
            nc.scalar.activation(rstd[:], mean_var[:, 1:2], FUNC.Abs_reciprocal_sqrt, bias=eps_col[:])
            normed = work.tile([BLOCK, C], F32, name="normed")
            nc.vector.tensor_scalar(normed[:], res_t[b][:], mean_var[:, 0:1], rstd[:], op0=SUBTRACT, op1=MULT)
            back = banks.tile([C, BLOCK], F32, name="back", tag="bank")
            nc.tensor.transpose(back[:], normed[:], ident[:])
            result = work.tile([C, BLOCK], F32, name="result")
            nc.scalar.activation(result[:], back[:], FUNC.Identity, scale=gamma_col, bias=beta_col)
            nc.sync.dma_start(out[:, lines], result[:])
